import numpy as np
import ml_dtypes


def mxq(x, axis, fmt="e4m3"):
    dtype, down = {"e4m3": (ml_dtypes.float8_e4m3fn, 7), "e5m2": (ml_dtypes.float8_e5m2, 14)}[fmt]
    v = np.moveaxis(np.asarray(x, np.float32).astype(ml_dtypes.bfloat16).astype(np.float64), axis, -1)
    blocks = v.reshape(v.shape[:-1] + (-1, 32))
    amax = np.abs(blocks).max(-1, keepdims=True)
    byte = np.maximum(np.where(amax > 0, np.frexp(amax)[1] - 1 + 127, 0) - down, 1)
    scale = np.exp2(byte - 127.0)
    codes = (blocks / scale).astype(np.float32).astype(dtype).astype(np.float64)
    return np.moveaxis((codes * scale).reshape(v.shape), -1, axis)


WIDE = False


def mx_kscale(k):
    if not WIDE:
        return np.ones(k)
    levels = np.array([10, -10, 5, -5, 0])
    a = np.random.permutation(np.resize(levels, k // 512 * 4)).reshape(k // 512, 4)
    idx = np.arange(k)
    return np.exp2(a[idx // 512, idx % 128 // 32])


BF16 = ml_dtypes.bfloat16


def bf(x):
    return np.asarray(x, np.float32).astype(BF16)


def f64(x):
    return np.asarray(x).astype(np.float64)


B, D_IN, D_HID, D_OUT = 4096, 512, 1024, 512
EPS = 1e-12
NORM_MAX = 16


def setup_inputs():
    s, t = mx_kscale(D_IN), mx_kscale(D_HID)
    return {
        "x": bf(np.random.standard_normal((B, D_IN))),
        "in_mean": bf(np.random.standard_normal(D_IN) * 0.1),
        "in_std": bf(np.random.uniform(0.5, 1.5, D_IN) / s),
        "out_mean": bf(np.random.standard_normal(D_OUT) * 0.1),
        "out_std": bf(np.random.uniform(0.5, 1.5, D_OUT)),
        "W1": bf(np.random.standard_normal((D_HID, D_IN)) / np.sqrt(D_IN) / s[None, :] * t[:, None]),
        "b1": bf(np.random.standard_normal(D_HID) * 0.1 * t),
        "W2": bf(np.random.standard_normal((D_OUT, D_HID)) * 0.85 / np.sqrt(D_HID) / t[None, :]),
        "b2": bf(np.random.standard_normal(D_OUT) * 0.1),
        "norm_max": NORM_MAX,
    }


def reference(x, in_mean, in_std, out_mean, out_std, W1, b1, W2, b2, norm_max):
    x, in_mean, in_std, out_mean, out_std = f64(x), f64(in_mean), f64(in_std), f64(out_mean), f64(out_std)
    norm_max = float(norm_max)
    x_copy = x[..., :D_OUT]
    xn = (x - in_mean) / in_std
    h = np.maximum((mxq(xn, 1, "e4m3") @ mxq(f64(W1), 1, "e4m3").T) + f64(b1), 0.0)
    res = (mxq(h, 1, "e4m3") @ mxq(f64(W2), 1, "e4m3").T) + f64(b2)
    norms = np.sqrt((res * res).sum(-1, keepdims=True))
    scale = norm_max / norms
    res = np.where(norms > norm_max, res * scale, res)
    res = res * out_std + out_mean - in_mean
    mapped = res + x_copy
    mnorm = np.sqrt((mapped * mapped).sum(-1, keepdims=True))
    return mapped / np.maximum(mnorm, EPS)

@@ -1,0 +1,243 @@
+from contextlib import ExitStack
+
+import concourse.mybir as mybir
+from concourse.masks import make_identity
+
+FLOPS = 2 * 4096 * (512 * 1024 + 1024 * 512)
+
+BF16 = mybir.dt.bfloat16
+F32 = mybir.dt.float32
+U32 = mybir.dt.uint32
+U8 = mybir.dt.uint8
+FP8X4 = mybir.dt.float8_e4m3fn_x4
+ALU = mybir.AluOpType
+ACT = mybir.ActivationFunctionType
+AX = mybir.AxisListType
+
+P = 128
+B = 4096
+D_IN = 512
+D_HID = 1024
+D_OUT = 512
+CH = 512
+NCH = B // CH
+NI = CH // P
+EPS = 1e-12
+
+
+def regroup(nc, dst, src):
+    nc.vector.tensor_copy(
+        out=dst.rearrange("p (c i) t -> p c t i", i=4),
+        in_=src.rearrange("p t (c i) -> p c t i", i=4),
+    )
+
+
+def quantise(nc, codes, scales, grouped):
+    nc.vector.quantize_mx(
+        out=codes.bitcast(FP8X4),
+        scales=scales,
+        in_=grouped.rearrange("p n t -> p (n t)"),
+    )
+
+
+def tile_mlp_t_kernel(tc, x, in_mean, in_std, out_mean, out_std, W1, b1, W2, b2, norm_max, out):
+    nc = tc.nc
+    nm2 = float(norm_max) * float(norm_max)
+    with ExitStack() as ctx:
+        keep = ctx.enter_context(tc.tile_pool(name="keep", bufs=1))
+        xpool = ctx.enter_context(tc.tile_pool(name="xpool", bufs=NCH))
+        work = ctx.enter_context(tc.tile_pool(name="work", bufs=2))
+        psum = ctx.enter_context(tc.psum_pool(name="psum", bufs=1))
+
+        warm = keep.tile([P, 1], F32)
+        nc.vector.memset(warm[:], 1.0)
+        warm2 = keep.tile([P, 1], F32)
+        nc.scalar.activation(out=warm2[:], in_=warm[:], func=ACT.Sqrt)
+
+        ident_bf = keep.tile([P, P], BF16)
+        make_identity(nc, ident_bf[:])
+        ident_f = keep.tile([P, P], F32)
+        make_identity(nc, ident_f[:])
+
+        sv = keep.tile([P, P], BF16)
+        nc.vector.memset(sv[:], 0.0)
+        nc.scalar.dma_start(out=sv[0:8, :], in_=b1.rearrange("(r c) -> r c", c=P))
+        nc.scalar.dma_start(out=sv[8:12, :], in_=in_mean.rearrange("(r c) -> r c", c=P))
+        nc.scalar.dma_start(out=sv[12:16, :], in_=in_std.rearrange("(r c) -> r c", c=P))
+        nc.scalar.dma_start(out=sv[16:20, :], in_=b2.rearrange("(r c) -> r c", c=P))
+        nc.scalar.dma_start(out=sv[20:24, :], in_=out_std.rearrange("(r c) -> r c", c=P))
+
+        W1n = keep.tile([P, 8, D_IN], BF16)
+        W1v = W1.rearrange("(m p) k -> p m k", p=P)
+        W2n = keep.tile([P, 4, D_HID], BF16)
+        xs_all = []
+        for c in range(NCH):
+            xs = xpool.tile([P, NI, D_IN], BF16)
+            xs_all.append(xs)
+
+        def load_x(c):
+            nc.sync.dma_start(
+                out=xs_all[c][:],
+                in_=x[c * CH:(c + 1) * CH, :].rearrange("(p i) k -> p i k", i=NI),
+            )
+
+        nc.sync.dma_start(out=W1n[:, 0:4, :], in_=W1v[:, 0:4, :])
+        load_x(0)
+        nc.sync.dma_start(out=W1n[:, 4:8, :], in_=W1v[:, 4:8, :])
+        nc.sync.dma_start(out=W2n[:], in_=W2.rearrange("(a p) k -> p a k", p=P))
+        load_x(1)
+        om_b = keep.tile([P, D_OUT], BF16)
+        im_b = keep.tile([P, D_OUT], BF16)
+        nc.sync.dma_start(out=om_b[:], in_=out_mean.partition_broadcast(P))
+        nc.sync.dma_start(out=im_b[:], in_=in_mean.partition_broadcast(P))
+        for c in range(2, NCH):
+            load_x(c)
+
+        svT = psum.tile([P, P], BF16, tag="qn", bufs=1)
+        nc.tensor.transpose(svT[:], sv[:], ident_bf[:])
+        svc = keep.tile([P, 24], F32)
+        nc.vector.tensor_copy(out=svc[:], in_=svT[:, 0:24])
+        rstd = keep.tile([P, 4], F32)
+        nc.vector.reciprocal(rstd[:], svc[:, 12:16])
+        sb2 = keep.tile([P, 4], F32)
+        nc.vector.tensor_mul(out=sb2[:], in0=svc[:, 16:20], in1=svc[:, 20:24])
+
+        gW1 = keep.tile([P, D_HID, 4], BF16, align_bytes=64)
+        W1q = keep.tile([P, D_HID], U32, align_bytes=64)
+        W1s = keep.tile([P, D_HID], U8, align_bytes=64)
+        for mm in range(4):
+            wt = psum.tile([P, 2, 4, P], BF16, tag=("l1" if mm % 2 == 0 else "pt"), bufs=2)
+            for m2 in range(2):
+                for t in range(4):
+                    nc.tensor.transpose(wt[:, m2, t, :], W1n[:, 2 * mm + m2, t * P:(t + 1) * P], ident_bf[:])
+            dst = gW1[:, 256 * mm:256 * (mm + 1), :].rearrange("p (m r) t -> p m r t", m=2)
+            src = wt[:].rearrange("p m t r -> p m r t")
+            if mm % 2 == 0:
+                nc.scalar.copy(out=dst, in_=src)
+            else:
+                nc.vector.tensor_copy(out=dst, in_=src)
+            if mm % 2 == 1:
+                h = mm // 2
+                quantise(nc, W1q[:, 512 * h:512 * (h + 1)], W1s[:, 512 * h:512 * (h + 1)], gW1[:, 512 * h:512 * (h + 1), :])
+
+        dm = keep.tile([P, D_OUT], F32)
+        W2q = keep.tile([P, 2, D_OUT], U32, align_bytes=64)
+        W2s = keep.tile([P, 2, D_OUT], U8, align_bytes=64)
+        gW2 = keep.tile([P, 2, D_OUT, 4], BF16, align_bytes=64)
+        junk = keep.tile([P, D_OUT], F32)
+
+        def prep_w2():
+            for g in range(2):
+                for jp in range(2):
+                    wt2 = psum.tile([P, 2, 4, P], BF16, tag=("l1" if jp == 0 else "pt"), bufs=2)
+                    for j2 in range(2):
+                        for t in range(4):
+                            k0 = 512 * g + P * t
+                            nc.tensor.transpose(wt2[:, j2, t, :], W2n[:, 2 * jp + j2, k0:k0 + P], ident_bf[:])
+                    dst2 = gW2[:, g, 256 * jp:256 * (jp + 1), :].rearrange("p (m r) t -> p m r t", m=2)
+                    src2 = wt2[:].rearrange("p m t r -> p m r t")
+                    if jp == 0:
+                        nc.scalar.copy(out=dst2, in_=src2)
+                    else:
+                        nc.vector.tensor_copy(out=dst2, in_=src2)
+                quantise(nc, W2q[:, g, :], W2s[:, g, :], gW2[:, g, :, :])
+
+        for c in range(NCH):
+            xs = xs_all[c]
+            sx = work.tile([P, 4, CH], BF16)
+            for th in range(2):
+                xT = psum.tile([P, 2, CH], BF16, tag="xT", bufs=2)
+                for t2 in range(2):
+                    t = 2 * th + t2
+                    for i in range(NI):
+                        nc.tensor.transpose(xT[:, t2, i * P:(i + 1) * P], xs[:, i, t * P:(t + 1) * P], ident_bf[:])
+                for t2 in range(2):
+                    t = 2 * th + t2
+                    nc.vector.tensor_scalar(
+                        out=sx[:, t, :], in0=xT[:, t2, :],
+                        scalar1=svc[:, 8 + t:9 + t], scalar2=rstd[:, t:t + 1],
+                        op0=ALU.subtract, op1=ALU.mult,
+                    )
+            gx = work.tile([P, CH, 4], BF16, align_bytes=64)
+            regroup(nc, gx[:], sx[:])
+            xq = work.tile([P, CH], U32, align_bytes=64)
+            xsc = work.tile([P, CH], U8, align_bytes=64)
+            quantise(nc, xq[:], xsc[:], gx[:])
+
+            sh = work.tile([P, 8, CH], BF16)
+            hq = work.tile([P, 2, CH], U32, align_bytes=64)
+            hs = work.tile([P, 2, CH], U8, align_bytes=64)
+            for g in range(2):
+                for t in range(4):
+                    m = 4 * g + t
+                    l1 = psum.tile([P, CH], F32, tag="l1", bufs=2)
+                    nc.tensor.matmul_mx(
+                        out=l1[:],
+                        lhsT=W1q[:, m * P:(m + 1) * P].bitcast(FP8X4), lhsT_scale=W1s[:, m * P:(m + 1) * P],
+                        rhs=xq[:].bitcast(FP8X4), rhs_scale=xsc[:],
+                        start=True, stop=True,
+                    )
+                    nc.scalar.activation(out=sh[:, m, :], in_=l1[:], func=ACT.Relu, bias=svc[:, m:m + 1], scale=1.0)
+                gh = work.tile([P, CH, 4], BF16, align_bytes=64, bufs=4)
+                regroup(nc, gh[:], sh[:, 4 * g:4 * g + 4, :])
+                quantise(nc, hq[:, g, :], hs[:, g, :], gh[:])
+
+            if c == 0:
+                prep_w2()
+                nc.vector.tensor_sub(out=dm[:], in0=om_b[:], in1=im_b[:])
+
+            Y = work.tile([P, NI, D_OUT], F32)
+            nc.vector.tensor_tensor(
+                out=Y[:], in0=xs[:], in1=dm[:].unsqueeze(1).to_broadcast([P, NI, D_OUT]), op=ALU.add,
+            )
+
+            qT = work.tile([P, 4, CH], F32)
+            r2T = work.tile([P, 4, CH], F32)
+            r2b = psum.tile([P, CH], F32, tag="r2", bufs=1)
+            for jt in range(4):
+                pt = psum.tile([P, CH], F32, tag="pt", bufs=2)
+                for g in range(2):
+                    nc.tensor.matmul_mx(
+                        out=pt[:],
+                        lhsT=W2q[:, g, jt * P:(jt + 1) * P].bitcast(FP8X4), lhsT_scale=W2s[:, g, jt * P:(jt + 1) * P],
+                        rhs=hq[:, g, :].bitcast(FP8X4), rhs_scale=hs[:, g, :],
+                        start=(g == 0), stop=(g == 1),
+                    )
+                nc.scalar.activation(out=r2T[:, jt, :], in_=pt[:], func=ACT.Square, bias=svc[:, 16 + jt:17 + jt], scale=1.0)
+                nc.scalar.activation(out=qT[:, jt, :], in_=pt[:], func=ACT.Identity, bias=sb2[:, jt:jt + 1], scale=svc[:, 20 + jt:21 + jt])
+                for i in range(NI):
+                    nc.tensor.matmul(
+                        out=r2b[:, i * P:(i + 1) * P], lhsT=r2T[:, jt, i * P:(i + 1) * P], rhs=ident_f[:],
+                        is_transpose=True, start=(jt == 0 and i == 0), stop=(jt == 3 and i == NI - 1),
+                    )
+            n2 = work.tile([P, NI], F32)
+            nc.vector.tensor_reduce(out=n2[:], in_=r2b[:].rearrange("p (i j) -> p i j", i=NI), axis=AX.X, op=ALU.add)
+            ncl = work.tile([P, NI], F32)
+            nc.vector.tensor_scalar_max(out=ncl[:], in0=n2[:], scalar1=nm2)
+            gam = work.tile([P, NI], F32)
+            nc.scalar.activation(out=gam[:], in_=ncl[:], func=ACT.Sqrt, scale=1.0 / nm2)
+            epsg = work.tile([P, NI], F32)
+            nc.vector.tensor_scalar_mul(out=epsg[:], in0=ncl[:], scalar1=EPS * EPS / nm2)
+
+            mp = work.tile([P, NI, D_OUT], F32)
+            m2 = work.tile([P, NI], F32)
+            for i in range(NI):
+                qn = psum.tile([P, D_OUT], F32, tag="qn", bufs=1)
+                for jt in range(4):
+                    nc.tensor.transpose(qn[:, jt * P:(jt + 1) * P], qT[:, jt, i * P:(i + 1) * P], ident_f[:])
+                nc.vector.scalar_tensor_tensor(
+                    out=mp[:, i, :], in0=Y[:, i, :], scalar=gam[:, i:i + 1], in1=qn[:], op0=ALU.mult, op1=ALU.add,
+                )
+                nc.scalar.activation(out=junk[:], in_=mp[:, i, :], func=ACT.Square, accum_out=m2[:, i:i + 1])
+            mcl = work.tile([P, NI], F32)
+            nc.vector.tensor_tensor(out=mcl[:], in0=m2[:], in1=epsg[:], op=ALU.max)
+            msq = work.tile([P, NI], F32)
+            nc.scalar.activation(out=msq[:], in_=mcl[:], func=ACT.Sqrt)
+            beta = work.tile([P, NI], F32)
+            nc.vector.reciprocal(beta[:], msq[:])
+            for i in range(NI):
+                nc.vector.tensor_scalar_mul(out=mp[:, i, :], in0=mp[:, i, :], scalar1=beta[:, i:i + 1])
+            nc.sync.dma_start(
+                out=out[c * CH:(c + 1) * CH, :].rearrange("(p i) j -> p i j", i=NI),
+                in_=mp[:],
+            )

@@ -23,6 +23,24 @@ CH = 512
 NCH = B // CH
 NI = CH // P
 EPS = 1e-12
+NPIECE = 3
+PERIOD = 8
+PIN = True
+
+STEPS = {
+    "w1t": [0, 1, 2, 3], "w1c": [1, 2, 3, 4], "w1q": [5, 7],
+    "w2t": [9, 11, 13, 15], "w2c": [10, 12, 14, 16], "w2q": [14, 18],
+    "xT": [0, 2], "X1": [1, 3], "X2": [4], "X3": [6],
+    "L1": [7, 8, 9, 10, 11, 12, 13, 14], "H1": [8, 9, 10, 11, 12, 13, 14, 15],
+    "H2": [14, 18], "H3": [16, 20],
+    "L2": [22, 24, 26, 28], "Sq": [23, 25, 27, 29], "Id": [24, 26, 28, 30], "r2": [25, 27, 29, 31],
+    "red": [32], "gam": [34], "split": [36], "gTp": [37], "gT": [39],
+    "qn": [41, 43, 45, 47], "stt": [42, 44, 46, 48], "Sqa": [44, 46, 48, 50],
+    "mcl": [52], "msq": [54], "rec": [56], "fin": [57, 58, 59, 60], "store": [61],
+}
+RANK = ["w1t", "L1", "L2", "r2", "qn", "gTp", "xT", "w2t", "rec", "mcl", "gT", "split", "fin", "store", "stt", "red",
+        "w1q", "w2q", "H3", "X3", "X1", "H2", "X2", "gam", "msq", "w1c", "H1", "Sq", "Id", "Sqa", "w2c"]
+ONCE = ["w1t", "w1c", "w1q", "w2t", "w2c", "w2q"]
 
 
 def regroup(nc, dst, src):
@@ -54,22 +72,29 @@ def tile_mlp_t_kernel(tc, x, in_mean, in_std, out_mean, out_std, W1, b1, W2, b2,
         warm2 = keep.tile([P, 1], F32)
         nc.scalar.activation(out=warm2[:], in_=warm[:], func=ACT.Sqrt)
 
+        sv = keep.tile([P, P], BF16)
+        nc.vector.memset(sv[:], 0.0)
+        nc.sync.dma_start(out=sv[0:8, :], in_=b1.rearrange("(r c) -> r c", c=P))
+        nc.sync.dma_start(out=sv[8:12, :], in_=in_mean.rearrange("(r c) -> r c", c=P))
+        nc.sync.dma_start(out=sv[12:16, :], in_=in_std.rearrange("(r c) -> r c", c=P))
+        nc.sync.dma_start(out=sv[16:20, :], in_=b2.rearrange("(r c) -> r c", c=P))
+        nc.sync.dma_start(out=sv[20:24, :], in_=out_std.rearrange("(r c) -> r c", c=P))
+
         ident_bf = keep.tile([P, P], BF16)
         make_identity(nc, ident_bf[:])
         ident_f = keep.tile([P, P], F32)
         make_identity(nc, ident_f[:])
 
-        sv = keep.tile([P, P], BF16)
-        nc.vector.memset(sv[:], 0.0)
-        nc.scalar.dma_start(out=sv[0:8, :], in_=b1.rearrange("(r c) -> r c", c=P))
-        nc.scalar.dma_start(out=sv[8:12, :], in_=in_mean.rearrange("(r c) -> r c", c=P))
-        nc.scalar.dma_start(out=sv[12:16, :], in_=in_std.rearrange("(r c) -> r c", c=P))
-        nc.scalar.dma_start(out=sv[16:20, :], in_=b2.rearrange("(r c) -> r c", c=P))
-        nc.scalar.dma_start(out=sv[20:24, :], in_=out_std.rearrange("(r c) -> r c", c=P))
-
-        W1n = keep.tile([P, 8, D_IN], BF16)
         W1v = W1.rearrange("(m p) k -> p m k", p=P)
-        W2n = keep.tile([P, 4, D_HID], BF16)
+        W1n = []
+        for mm in range(4):
+            w1piece = keep.tile([P, 2, D_IN], BF16, name="w1piece%d" % mm)
+            W1n.append(w1piece)
+        W2v = W2.rearrange("(a p) k -> p a k", p=P)
+        W2n = []
+        for jp in range(2):
+            w2piece = keep.tile([P, 2, D_HID], BF16, name="w2piece%d" % jp)
+            W2n.append(w2piece)
         xs_all = []
         for c in range(NCH):
             xs = xpool.tile([P, NI, D_IN], BF16)
@@ -81,19 +106,32 @@ def tile_mlp_t_kernel(tc, x, in_mean, in_std, out_mean, out_std, W1, b1, W2, b2,
                 in_=x[c * CH:(c + 1) * CH, :].rearrange("(p i) k -> p i k", i=NI),
             )
 
-        nc.sync.dma_start(out=W1n[:, 0:4, :], in_=W1v[:, 0:4, :])
+        def load_w1(mm):
+            nc.sync.dma_start(out=W1n[mm][:], in_=W1v[:, 2 * mm:2 * mm + 2, :])
+
+        load_w1(0)
         load_x(0)
-        nc.sync.dma_start(out=W1n[:, 4:8, :], in_=W1v[:, 4:8, :])
-        nc.sync.dma_start(out=W2n[:], in_=W2.rearrange("(a p) k -> p a k", p=P))
+        load_w1(1)
+        load_w1(2)
+        load_w1(3)
         load_x(1)
-        om_b = keep.tile([P, D_OUT], BF16)
-        im_b = keep.tile([P, D_OUT], BF16)
-        nc.sync.dma_start(out=om_b[:], in_=out_mean.partition_broadcast(P))
-        nc.sync.dma_start(out=im_b[:], in_=in_mean.partition_broadcast(P))
+        for jp in range(2):
+            nc.sync.dma_start(out=W2n[jp][:], in_=W2v[:, 2 * jp:2 * jp + 2, :])
         for c in range(2, NCH):
             load_x(c)
 
-        svT = psum.tile([P, P], BF16, tag="qn", bufs=1)
+        shift = keep.tile([P, NI, D_OUT], BF16)
+        nc.vector.memset(shift[:], 0.0)
+        for i in range(NI):
+            nc.sync.dma_start(out=shift[4 * i:4 * i + 4, i, :], in_=out_mean.partition_broadcast(4))
+            nc.sync.dma_start(out=shift[32 + 4 * i:32 + 4 * i + 4, i, :], in_=in_mean.partition_broadcast(4))
+        gcols = []
+        for bb in range(2):
+            gc = keep.tile([P, P], BF16, name="gcols%d" % bb)
+            nc.vector.memset(gc[:], 0.0)
+            gcols.append(gc)
+
+        svT = psum.tile([P, P], BF16, tag="qn", bufs=2)
         nc.tensor.transpose(svT[:], sv[:], ident_bf[:])
         svc = keep.tile([P, 24], F32)
         nc.vector.tensor_copy(out=svc[:], in_=svT[:, 0:24])
@@ -105,139 +143,240 @@ def tile_mlp_t_kernel(tc, x, in_mean, in_std, out_mean, out_std, W1, b1, W2, b2,
         gW1 = keep.tile([P, D_HID, 4], BF16, align_bytes=64)
         W1q = keep.tile([P, D_HID], U32, align_bytes=64)
         W1s = keep.tile([P, D_HID], U8, align_bytes=64)
-        for mm in range(4):
-            wt = psum.tile([P, 2, 4, P], BF16, tag=("l1" if mm % 2 == 0 else "pt"), bufs=2)
-            for m2 in range(2):
-                for t in range(4):
-                    nc.tensor.transpose(wt[:, m2, t, :], W1n[:, 2 * mm + m2, t * P:(t + 1) * P], ident_bf[:])
-            dst = gW1[:, 256 * mm:256 * (mm + 1), :].rearrange("p (m r) t -> p m r t", m=2)
-            src = wt[:].rearrange("p m t r -> p m r t")
-            if mm % 2 == 0:
-                nc.scalar.copy(out=dst, in_=src)
-            else:
-                nc.vector.tensor_copy(out=dst, in_=src)
-            if mm % 2 == 1:
-                h = mm // 2
-                quantise(nc, W1q[:, 512 * h:512 * (h + 1)], W1s[:, 512 * h:512 * (h + 1)], gW1[:, 512 * h:512 * (h + 1), :])
-
-        dm = keep.tile([P, D_OUT], F32)
         W2q = keep.tile([P, 2, D_OUT], U32, align_bytes=64)
         W2s = keep.tile([P, 2, D_OUT], U8, align_bytes=64)
         gW2 = keep.tile([P, 2, D_OUT, 4], BF16, align_bytes=64)
         junk = keep.tile([P, D_OUT], F32)
 
-        def prep_w2():
-            for g in range(2):
-                for jp in range(2):
-                    wt2 = psum.tile([P, 2, 4, P], BF16, tag=("l1" if jp == 0 else "pt"), bufs=2)
-                    for j2 in range(2):
-                        for t in range(4):
-                            k0 = 512 * g + P * t
-                            nc.tensor.transpose(wt2[:, j2, t, :], W2n[:, 2 * jp + j2, k0:k0 + P], ident_bf[:])
-                    dst2 = gW2[:, g, 256 * jp:256 * (jp + 1), :].rearrange("p (m r) t -> p m r t", m=2)
-                    src2 = wt2[:].rearrange("p m t r -> p m r t")
-                    if jp == 0:
-                        nc.scalar.copy(out=dst2, in_=src2)
-                    else:
-                        nc.vector.tensor_copy(out=dst2, in_=src2)
-                quantise(nc, W2q[:, g, :], W2s[:, g, :], gW2[:, g, :, :])
+        T = {}
 
-        for c in range(NCH):
-            xs = xs_all[c]
-            sx = work.tile([P, 4, CH], BF16)
-            for th in range(2):
-                xT = psum.tile([P, 2, CH], BF16, tag="xT", bufs=2)
-                for t2 in range(2):
-                    t = 2 * th + t2
-                    for i in range(NI):
-                        nc.tensor.transpose(xT[:, t2, i * P:(i + 1) * P], xs[:, i, t * P:(t + 1) * P], ident_bf[:])
-                for t2 in range(2):
-                    t = 2 * th + t2
-                    nc.vector.tensor_scalar(
-                        out=sx[:, t, :], in0=xT[:, t2, :],
-                        scalar1=svc[:, 8 + t:9 + t], scalar2=rstd[:, t:t + 1],
-                        op0=ALU.subtract, op1=ALU.mult,
-                    )
-            gx = work.tile([P, CH, 4], BF16, align_bytes=64)
-            regroup(nc, gx[:], sx[:])
-            xq = work.tile([P, CH], U32, align_bytes=64)
-            xsc = work.tile([P, CH], U8, align_bytes=64)
-            quantise(nc, xq[:], xsc[:], gx[:])
-
-            sh = work.tile([P, 8, CH], BF16)
-            hq = work.tile([P, 2, CH], U32, align_bytes=64)
-            hs = work.tile([P, 2, CH], U8, align_bytes=64)
-            for g in range(2):
+        def e_w1t(c, mm):
+            wt = psum.tile([P, 2, 4, P], BF16, tag=("l1" if mm % 2 == 0 else "pt"), bufs=2)
+            T["wt", mm] = wt
+            for m2 in range(2):
                 for t in range(4):
-                    m = 4 * g + t
-                    l1 = psum.tile([P, CH], F32, tag="l1", bufs=2)
-                    nc.tensor.matmul_mx(
-                        out=l1[:],
-                        lhsT=W1q[:, m * P:(m + 1) * P].bitcast(FP8X4), lhsT_scale=W1s[:, m * P:(m + 1) * P],
-                        rhs=xq[:].bitcast(FP8X4), rhs_scale=xsc[:],
-                        start=True, stop=True,
-                    )
-                    nc.scalar.activation(out=sh[:, m, :], in_=l1[:], func=ACT.Relu, bias=svc[:, m:m + 1], scale=1.0)
-                gh = work.tile([P, CH, 4], BF16, align_bytes=64, bufs=4)
-                regroup(nc, gh[:], sh[:, 4 * g:4 * g + 4, :])
-                quantise(nc, hq[:, g, :], hs[:, g, :], gh[:])
+                    nc.tensor.transpose(wt[:, m2, t, :], W1n[mm][:, m2, t * P:(t + 1) * P], ident_bf[:])
 
-            if c == 0:
-                prep_w2()
-                nc.vector.tensor_sub(out=dm[:], in0=om_b[:], in1=im_b[:])
+        def e_w1c(c, mm):
+            dst = gW1[:, 256 * mm:256 * (mm + 1), :].rearrange("p (m r) t -> p m r t", m=2)
+            nc.scalar.copy(out=dst, in_=T["wt", mm][:].rearrange("p m t r -> p m r t"))
 
-            Y = work.tile([P, NI, D_OUT], F32)
-            nc.vector.tensor_tensor(
-                out=Y[:], in0=xs[:], in1=dm[:].unsqueeze(1).to_broadcast([P, NI, D_OUT]), op=ALU.add,
+        def e_w1q(c, h):
+            quantise(nc, W1q[:, 512 * h:512 * (h + 1)], W1s[:, 512 * h:512 * (h + 1)], gW1[:, 512 * h:512 * (h + 1), :])
+
+        def e_w2t(c, u):
+            g, jp = u // 2, u % 2
+            wt2 = psum.tile([P, 2, 4, P], BF16, tag="pt", bufs=2)
+            T["wt2", u] = wt2
+            for j2 in range(2):
+                for t in range(4):
+                    k0 = 512 * g + P * t
+                    nc.tensor.transpose(wt2[:, j2, t, :], W2n[jp][:, j2, k0:k0 + P], ident_bf[:])
+
+        def e_w2c(c, u):
+            g, jp = u // 2, u % 2
+            dst2 = gW2[:, g, 256 * jp:256 * (jp + 1), :].rearrange("p (m r) t -> p m r t", m=2)
+            src2 = T["wt2", u][:].rearrange("p m t r -> p m r t")
+            if jp == 0:
+                nc.scalar.copy(out=dst2, in_=src2)
+            else:
+                nc.vector.tensor_copy(out=dst2, in_=src2)
+
+        def e_w2q(c, g):
+            quantise(nc, W2q[:, g, :], W2s[:, g, :], gW2[:, g, :, :])
+            if g == 1:
+                nc.vector.tensor_scalar_mul(out=shift[32:64, :, :], in0=shift[32:64, :, :], scalar1=-1.0)
+
+        def e_xT(c, th):
+            xT = psum.tile([P, 2, CH], BF16, tag="xT", bufs=1)
+            T["xT", c, th] = xT
+            for t2 in range(2):
+                t = 2 * th + t2
+                for i in range(NI):
+                    nc.tensor.transpose(xT[:, t2, i * P:(i + 1) * P], xs_all[c][:, i, t * P:(t + 1) * P], ident_bf[:])
+
+        def e_X1(c, th):
+            if th == 0:
+                sx = work.tile([P, 4, CH], BF16, tag="sx", bufs=2)
+                T["sx", c] = sx
+            for t2 in range(2):
+                t = 2 * th + t2
+                nc.vector.tensor_scalar(
+                    out=T["sx", c][:, t, :], in0=T["xT", c, th][:, t2, :],
+                    scalar1=svc[:, 8 + t:9 + t], scalar2=rstd[:, t:t + 1],
+                    op0=ALU.subtract, op1=ALU.mult,
+                )
+
+        def e_X2(c, k):
+            gx = work.tile([P, CH, 4], BF16, tag="gx", bufs=2, align_bytes=64)
+            T["gx", c] = gx
+            regroup(nc, gx[:], T["sx", c][:])
+
+        def e_X3(c, k):
+            xq = work.tile([P, CH], U32, tag="xq", bufs=2, align_bytes=64)
+            xsc = work.tile([P, CH], U8, tag="xsc", bufs=2, align_bytes=64)
+            T["xq", c] = xq
+            T["xsc", c] = xsc
+            quantise(nc, xq[:], xsc[:], T["gx", c][:])
+
+        def e_L1(c, m):
+            l1 = psum.tile([P, CH], F32, tag="l1", bufs=2)
+            T["l1", c, m] = l1
+            nc.tensor.matmul_mx(
+                out=l1[:],
+                lhsT=W1q[:, m * P:(m + 1) * P].bitcast(FP8X4), lhsT_scale=W1s[:, m * P:(m + 1) * P],
+                rhs=T["xq", c][:].bitcast(FP8X4), rhs_scale=T["xsc", c][:],
+                start=True, stop=True,
             )
 
-            qT = work.tile([P, 4, CH], F32)
-            r2T = work.tile([P, 4, CH], F32)
-            r2b = psum.tile([P, CH], F32, tag="r2", bufs=1)
-            for jt in range(4):
-                pt = psum.tile([P, CH], F32, tag="pt", bufs=2)
-                for g in range(2):
-                    nc.tensor.matmul_mx(
-                        out=pt[:],
-                        lhsT=W2q[:, g, jt * P:(jt + 1) * P].bitcast(FP8X4), lhsT_scale=W2s[:, g, jt * P:(jt + 1) * P],
-                        rhs=hq[:, g, :].bitcast(FP8X4), rhs_scale=hs[:, g, :],
-                        start=(g == 0), stop=(g == 1),
-                    )
-                nc.scalar.activation(out=r2T[:, jt, :], in_=pt[:], func=ACT.Square, bias=svc[:, 16 + jt:17 + jt], scale=1.0)
-                nc.scalar.activation(out=qT[:, jt, :], in_=pt[:], func=ACT.Identity, bias=sb2[:, jt:jt + 1], scale=svc[:, 20 + jt:21 + jt])
-                for i in range(NI):
-                    nc.tensor.matmul(
-                        out=r2b[:, i * P:(i + 1) * P], lhsT=r2T[:, jt, i * P:(i + 1) * P], rhs=ident_f[:],
-                        is_transpose=True, start=(jt == 0 and i == 0), stop=(jt == 3 and i == NI - 1),
-                    )
-            n2 = work.tile([P, NI], F32)
-            nc.vector.tensor_reduce(out=n2[:], in_=r2b[:].rearrange("p (i j) -> p i j", i=NI), axis=AX.X, op=ALU.add)
-            ncl = work.tile([P, NI], F32)
-            nc.vector.tensor_scalar_max(out=ncl[:], in0=n2[:], scalar1=nm2)
-            gam = work.tile([P, NI], F32)
-            nc.scalar.activation(out=gam[:], in_=ncl[:], func=ACT.Sqrt, scale=1.0 / nm2)
-            epsg = work.tile([P, NI], F32)
-            nc.vector.tensor_scalar_mul(out=epsg[:], in0=ncl[:], scalar1=EPS * EPS / nm2)
+        def e_H1(c, m):
+            if m % 4 == 0:
+                sh = work.tile([P, 4, CH], BF16, tag="sh", bufs=3)
+                T["sh", c, m // 4] = sh
+            nc.scalar.activation(out=T["sh", c, m // 4][:, m % 4, :], in_=T["l1", c, m][:], func=ACT.Relu,
+                                 bias=svc[:, m:m + 1], scale=1.0)
 
-            mp = work.tile([P, NI, D_OUT], F32)
-            m2 = work.tile([P, NI], F32)
-            for i in range(NI):
-                qn = psum.tile([P, D_OUT], F32, tag="qn", bufs=1)
-                for jt in range(4):
-                    nc.tensor.transpose(qn[:, jt * P:(jt + 1) * P], qT[:, jt, i * P:(i + 1) * P], ident_f[:])
-                nc.vector.scalar_tensor_tensor(
-                    out=mp[:, i, :], in0=Y[:, i, :], scalar=gam[:, i:i + 1], in1=qn[:], op0=ALU.mult, op1=ALU.add,
+        def e_H2(c, g):
+            gh = work.tile([P, CH, 4], BF16, tag="gh", bufs=2, align_bytes=64)
+            T["gh", c, g] = gh
+            regroup(nc, gh[:], T["sh", c, g][:])
+
+        def e_H3(c, g):
+            if g == 0:
+                hq = work.tile([P, 2, CH], U32, tag="hq", bufs=2, align_bytes=64)
+                hs = work.tile([P, 2, CH], U8, tag="hs", bufs=2, align_bytes=64)
+                T["hq", c] = hq
+                T["hs", c] = hs
+            quantise(nc, T["hq", c][:, g, :], T["hs", c][:, g, :], T["gh", c, g][:])
+
+        def e_L2(c, jt):
+            pt = psum.tile([P, CH], F32, tag="pt", bufs=2)
+            T["pt", c, jt] = pt
+            for g in range(2):
+                nc.tensor.matmul_mx(
+                    out=pt[:],
+                    lhsT=W2q[:, g, jt * P:(jt + 1) * P].bitcast(FP8X4), lhsT_scale=W2s[:, g, jt * P:(jt + 1) * P],
+                    rhs=T["hq", c][:, g, :].bitcast(FP8X4), rhs_scale=T["hs", c][:, g, :],
+                    start=(g == 0), stop=(g == 1),
                 )
-                nc.scalar.activation(out=junk[:], in_=mp[:, i, :], func=ACT.Square, accum_out=m2[:, i:i + 1])
-            mcl = work.tile([P, NI], F32)
-            nc.vector.tensor_tensor(out=mcl[:], in0=m2[:], in1=epsg[:], op=ALU.max)
-            msq = work.tile([P, NI], F32)
-            nc.scalar.activation(out=msq[:], in_=mcl[:], func=ACT.Sqrt)
-            beta = work.tile([P, NI], F32)
-            nc.vector.reciprocal(beta[:], msq[:])
+
+        def e_Sq(c, jt):
+            r2T = work.tile([P, CH], F32, tag="r2T", bufs=3)
+            T["r2T", c, jt] = r2T
+            nc.scalar.activation(out=r2T[:], in_=T["pt", c, jt][:], func=ACT.Square, bias=svc[:, 16 + jt:17 + jt], scale=1.0)
+
+        def e_Id(c, jt):
+            if jt == 0:
+                qT = work.tile([P, 4, CH], F32, tag="qT", bufs=4)
+                T["qT", c] = qT
+            nc.scalar.activation(out=T["qT", c][:, jt, :], in_=T["pt", c, jt][:], func=ACT.Identity,
+                                 bias=sb2[:, jt:jt + 1], scale=svc[:, 20 + jt:21 + jt])
+
+        def e_r2(c, jt):
+            if jt == 0:
+                r2b = psum.tile([P, CH], F32, tag="r2", bufs=1)
+                T["r2b", c] = r2b
             for i in range(NI):
-                nc.vector.tensor_scalar_mul(out=mp[:, i, :], in0=mp[:, i, :], scalar1=beta[:, i:i + 1])
+                nc.tensor.matmul(
+                    out=T["r2b", c][:, i * P:(i + 1) * P], lhsT=T["r2T", c, jt][:, i * P:(i + 1) * P], rhs=ident_f[:],
+                    is_transpose=True, start=(jt == 0 and i == 0), stop=(jt == 3 and i == NI - 1),
+                )
+
+        def e_red(c, k):
+            n2 = work.tile([P, NI], F32, tag="n2", bufs=4)
+            nc.vector.tensor_reduce(out=n2[:], in_=T["r2b", c][:].rearrange("p (i j) -> p i j", i=NI), axis=AX.X, op=ALU.add)
+            ncl = work.tile([P, NI], F32, tag="ncl", bufs=4)
+            T["ncl", c] = ncl
+            nc.vector.tensor_scalar_max(out=ncl[:], in0=n2[:], scalar1=nm2)
+
+        def e_gam(c, k):
+            gam = work.tile([P, NI], F32, tag="gam", bufs=4)
+            T["gam", c] = gam
+            nc.scalar.activation(out=gam[:], in_=T["ncl", c][:], func=ACT.Sqrt, scale=1.0 / nm2)
+
+        def e_split(c, k):
+            gview = gcols[c % 2][:, 0:64].rearrange("p (s i a) -> p s i a", s=2, a=4)
+            rest = T["gam", c]
+            for a in range(NPIECE):
+                nc.vector.tensor_copy(out=gview[:, :, 0:NI, a], in_=rest[:].unsqueeze(1).to_broadcast([P, 2, NI]))
+                if a < NPIECE - 1:
+                    nrest = work.tile([P, NI], F32, tag="rest%d" % a, bufs=2)
+                    nc.vector.tensor_sub(out=nrest[:], in0=rest[:], in1=gview[:, 0, 0:NI, a])
+                    rest = nrest
+
+        def e_gTp(c, k):
+            gTp = psum.tile([P, P], BF16, tag="xT", bufs=1)
+            T["gTp", c] = gTp
+            nc.tensor.transpose(gTp[:], gcols[c % 2][:], ident_bf[:])
+
+        def e_gT(c, k):
+            gT = work.tile([P, P], BF16, tag="gT", bufs=2)
+            T["gT", c] = gT
+            nc.vector.tensor_copy(out=gT[:], in_=T["gTp", c][:])
+
+        def e_qn(c, i):
+            qn = psum.tile([P, D_OUT], F32, tag="qn", bufs=2)
+            T["qn", c, i] = qn
+            for jt in range(4):
+                nc.tensor.matmul(
+                    out=qn[:, jt * P:(jt + 1) * P], lhsT=T["qT", c][:, jt, i * P:(i + 1) * P], rhs=ident_f[:],
+                    is_transpose=True, start=(jt == 0), stop=False,
+                )
+            nc.tensor.matmul(out=qn[:], lhsT=T["gT", c][:], rhs=shift[:, i, :], start=False, stop=True)
+
+        def e_stt(c, i):
+            if i == 0:
+                mp = work.tile([P, NI, D_OUT], F32, tag="mp", bufs=3)
+                m2 = work.tile([P, NI], F32, tag="m2", bufs=3)
+                T["mp", c] = mp
+                T["m2", c] = m2
+            nc.vector.scalar_tensor_tensor(
+                out=T["mp", c][:, i, :], in0=xs_all[c][:, i, :], scalar=T["gam", c][:, i:i + 1], in1=T["qn", c, i][:],
+                op0=ALU.mult, op1=ALU.add,
+            )
+
+        def e_Sqa(c, i):
+            nc.scalar.activation(out=junk[:], in_=T["mp", c][:, i, :], func=ACT.Square, accum_out=T["m2", c][:, i:i + 1])
+
+        def e_mcl(c, k):
+            mcl = work.tile([P, NI], F32, tag="mcl", bufs=2)
+            T["mcl", c] = mcl
+            nc.vector.scalar_tensor_tensor(
+                out=mcl[:], in0=T["ncl", c][:], scalar=EPS * EPS / nm2, in1=T["m2", c][:], op0=ALU.mult, op1=ALU.max,
+            )
+
+        def e_msq(c, k):
+            msq = work.tile([P, NI], F32, tag="msq", bufs=2)
+            T["msq", c] = msq
+            nc.scalar.activation(out=msq[:], in_=T["mcl", c][:], func=ACT.Sqrt)
+
+        def e_rec(c, k):
+            beta = work.tile([P, NI], F32, tag="beta", bufs=2)
+            T["beta", c] = beta
+            nc.vector.reciprocal(beta[:], T["msq", c][:])
+
+        def e_fin(c, i):
+            nc.vector.tensor_scalar_mul(out=T["mp", c][:, i, :], in0=T["mp", c][:, i, :], scalar1=T["beta", c][:, i:i + 1])
+
+        def e_store(c, k):
             nc.sync.dma_start(
                 out=out[c * CH:(c + 1) * CH, :].rearrange("(p i) j -> p i j", i=NI),
-                in_=mp[:],
+                in_=T["mp", c][:],
             )
+
+        emit = {
+            "w1t": e_w1t, "w1c": e_w1c, "w1q": e_w1q, "w2t": e_w2t, "w2c": e_w2c, "w2q": e_w2q,
+            "xT": e_xT, "X1": e_X1, "X2": e_X2, "X3": e_X3, "L1": e_L1, "H1": e_H1, "H2": e_H2, "H3": e_H3,
+            "L2": e_L2, "Sq": e_Sq, "Id": e_Id, "r2": e_r2, "red": e_red, "gam": e_gam, "split": e_split,
+            "gTp": e_gTp, "gT": e_gT, "qn": e_qn, "stt": e_stt, "Sqa": e_Sqa, "mcl": e_mcl, "msq": e_msq,
+            "rec": e_rec, "fin": e_fin, "store": e_store,
+        }
+        events = []
+        for kind in RANK:
+            for c in range(1 if kind in ONCE else NCH):
+                for k in range(len(STEPS[kind])):
+                    events.append((PERIOD * c + STEPS[kind][k], RANK.index(kind), c, k, kind))
+        if PIN:
+            ctx.enter_context(tc.manual_schedule())
+        for ev in sorted(events):
+            emit[ev[4]](ev[2], ev[3])

@@ -34,11 +34,11 @@ STEPS = {
     "L1": [7, 8, 9, 10, 11, 12, 13, 14], "H1": [8, 9, 10, 11, 12, 13, 14, 15],
     "H2": [14, 18], "H3": [16, 20],
     "L2": [22, 24, 26, 28], "Sq": [23, 25, 27, 29], "Id": [24, 26, 28, 30], "r2": [25, 27, 29, 31],
-    "red": [32], "gam": [34], "split": [36], "gTp": [37], "gT": [39],
+    "red": [32], "ncl": [33], "gam": [34], "split": [35], "gTp": [37], "gT": [39],
     "qn": [41, 43, 45, 47], "stt": [42, 44, 46, 48], "Sqa": [44, 46, 48, 50],
     "mcl": [52], "msq": [54], "rec": [56], "fin": [57, 58, 59, 60], "store": [61],
 }
-RANK = ["w1t", "L1", "L2", "r2", "qn", "gTp", "xT", "w2t", "rec", "mcl", "gT", "split", "fin", "store", "stt", "red",
+RANK = ["w1t", "L1", "L2", "r2", "qn", "gTp", "xT", "w2t", "rec", "mcl", "gT", "split", "fin", "store", "stt", "red", "ncl",
         "w1q", "w2q", "H3", "X3", "X1", "H2", "X2", "gam", "msq", "w1c", "H1", "Sq", "Id", "Sqa", "w2c"]
 ONCE = ["w1t", "w1c", "w1q", "w2t", "w2c", "w2q"]
 
@@ -284,10 +284,13 @@ def tile_mlp_t_kernel(tc, x, in_mean, in_std, out_mean, out_std, W1, b1, W2, b2,
 
         def e_red(c, k):
             n2 = work.tile([P, NI], F32, tag="n2", bufs=4)
+            T["n2", c] = n2
             nc.vector.tensor_reduce(out=n2[:], in_=T["r2b", c][:].rearrange("p (i j) -> p i j", i=NI), axis=AX.X, op=ALU.add)
+
+        def e_ncl(c, k):
             ncl = work.tile([P, NI], F32, tag="ncl", bufs=4)
             T["ncl", c] = ncl
-            nc.vector.tensor_scalar_max(out=ncl[:], in0=n2[:], scalar1=nm2)
+            nc.gpsimd.tensor_scalar_max(out=ncl[:], in0=T["n2", c][:], scalar1=nm2)
 
         def e_gam(c, k):
             gam = work.tile([P, NI], F32, tag="gam", bufs=4)
@@ -298,10 +301,10 @@ def tile_mlp_t_kernel(tc, x, in_mean, in_std, out_mean, out_std, W1, b1, W2, b2,
             gview = gcols[c % 2][:, 0:64].rearrange("p (s i a) -> p s i a", s=2, a=4)
             rest = T["gam", c]
             for a in range(NPIECE):
-                nc.vector.tensor_copy(out=gview[:, :, 0:NI, a], in_=rest[:].unsqueeze(1).to_broadcast([P, 2, NI]))
+                nc.gpsimd.tensor_copy(out=gview[:, :, 0:NI, a], in_=rest[:].unsqueeze(1).to_broadcast([P, 2, NI]))
                 if a < NPIECE - 1:
                     nrest = work.tile([P, NI], F32, tag="rest%d" % a, bufs=2)
-                    nc.vector.tensor_sub(out=nrest[:], in0=rest[:], in1=gview[:, 0, 0:NI, a])
+                    nc.gpsimd.tensor_sub(out=nrest[:], in0=rest[:], in1=gview[:, 0, 0:NI, a])
                     rest = nrest
 
         def e_gTp(c, k):
@@ -367,7 +370,7 @@ def tile_mlp_t_kernel(tc, x, in_mean, in_std, out_mean, out_std, W1, b1, W2, b2,
         emit = {
             "w1t": e_w1t, "w1c": e_w1c, "w1q": e_w1q, "w2t": e_w2t, "w2c": e_w2c, "w2q": e_w2q,
             "xT": e_xT, "X1": e_X1, "X2": e_X2, "X3": e_X3, "L1": e_L1, "H1": e_H1, "H2": e_H2, "H3": e_H3,
-            "L2": e_L2, "Sq": e_Sq, "Id": e_Id, "r2": e_r2, "red": e_red, "gam": e_gam, "split": e_split,
+            "L2": e_L2, "Sq": e_Sq, "Id": e_Id, "r2": e_r2, "red": e_red, "ncl": e_ncl, "gam": e_gam, "split": e_split,
             "gTp": e_gTp, "gT": e_gT, "qn": e_qn, "stt": e_stt, "Sqa": e_Sqa, "mcl": e_mcl, "msq": e_msq,
             "rec": e_rec, "fin": e_fin, "store": e_store,
         }

@@ -26,6 +26,7 @@ EPS = 1e-12
 NPIECE = 3
 PERIOD = 8
 PIN = True
+ID_ON_VECTOR = [3]
 
 STEPS = {
     "w1t": [0, 1, 2, 3], "w1c": [1, 2, 3, 4], "w1q": [5, 7],
@@ -34,7 +35,7 @@ STEPS = {
     "L1": [7, 8, 9, 10, 11, 12, 13, 14], "H1": [8, 9, 10, 11, 12, 13, 14, 15],
     "H2": [14, 18], "H3": [16, 20],
     "L2": [22, 24, 26, 28], "Sq": [23, 25, 27, 29], "Id": [24, 26, 28, 30], "r2": [25, 27, 29, 31],
-    "red": [32], "ncl": [33], "gam": [34], "split": [35], "gTp": [37], "gT": [39],
+    "red": [32], "ncl": [33], "gam": [35], "split": [36], "gTp": [38], "gT": [39],
     "qn": [41, 43, 45, 47], "stt": [42, 44, 46, 48], "Sqa": [44, 46, 48, 50],
     "mcl": [52], "msq": [54], "rec": [56], "fin": [57, 58, 59, 60], "store": [61],
 }
@@ -269,8 +270,14 @@ def tile_mlp_t_kernel(tc, x, in_mean, in_std, out_mean, out_std, W1, b1, W2, b2,
             if jt == 0:
                 qT = work.tile([P, 4, CH], F32, tag="qT", bufs=4)
                 T["qT", c] = qT
-            nc.scalar.activation(out=T["qT", c][:, jt, :], in_=T["pt", c, jt][:], func=ACT.Identity,
-                                 bias=sb2[:, jt:jt + 1], scale=svc[:, 20 + jt:21 + jt])
+            if jt in ID_ON_VECTOR:
+                nc.vector.tensor_scalar(
+                    out=T["qT", c][:, jt, :], in0=T["pt", c, jt][:],
+                    scalar1=svc[:, 20 + jt:21 + jt], scalar2=sb2[:, jt:jt + 1], op0=ALU.mult, op1=ALU.add,
+                )
+            else:
+                nc.scalar.activation(out=T["qT", c][:, jt, :], in_=T["pt", c, jt][:], func=ACT.Identity,
+                                     bias=sb2[:, jt:jt + 1], scale=svc[:, 20 + jt:21 + jt])
 
         def e_r2(c, jt):
             if jt == 0:
@@ -359,7 +366,10 @@ def tile_mlp_t_kernel(tc, x, in_mean, in_std, out_mean, out_std, W1, b1, W2, b2,
             nc.vector.reciprocal(beta[:], T["msq", c][:])
 
         def e_fin(c, i):
-            nc.vector.tensor_scalar_mul(out=T["mp", c][:, i, :], in0=T["mp", c][:, i, :], scalar1=T["beta", c][:, i:i + 1])
+            nc.gpsimd.tensor_scalar(
+                out=T["mp", c][:, i, :], in0=T["mp", c][:, i, :], scalar1=T["beta", c][:, i:i + 1], scalar2=0.0,
+                op0=ALU.mult, op1=ALU.add,
+            )
 
         def e_store(c, k):
             nc.sync.dma_start(

@@ -27,9 +27,10 @@ NPIECE = 3
 PERIOD = 8
 PIN = True
 ID_ON_VECTOR = [3]
+VFIN = [NCH - 2, NCH - 1]
 
 STEPS = {
-    "w1t": [0, 1, 2, 3], "w1c": [1, 2, 3, 4], "w1q": [5, 7],
+    "sv": [0], "w1t": [0, 1, 2, 3], "w1c": [1, 2, 3, 4], "w1q": [5, 7],
     "w2t": [9, 11, 13, 15], "w2c": [10, 12, 14, 16], "w2q": [14, 18],
     "xT": [0, 2], "X1": [1, 3], "X2": [4], "X3": [6],
     "L1": [7, 8, 9, 10, 11, 12, 13, 14], "H1": [8, 9, 10, 11, 12, 13, 14, 15],
@@ -37,11 +38,11 @@ STEPS = {
     "L2": [22, 24, 26, 28], "Sq": [23, 25, 27, 29], "Id": [24, 26, 28, 30], "r2": [25, 27, 29, 31],
     "red": [32], "ncl": [33], "gam": [35], "split": [36], "gTp": [38], "gT": [39],
     "qn": [41, 43, 45, 47], "stt": [42, 44, 46, 48], "Sqa": [44, 46, 48, 50],
-    "mcl": [52], "msq": [54], "rec": [56], "fin": [57, 58, 59, 60], "store": [61],
+    "mcl": [52], "msq": [54], "rec": [56], "fin": [61, 62, 63, 64], "store": [65], "finV": [57, 58, 59, 60], "storeV": [61],
 }
-RANK = ["w1t", "L1", "L2", "r2", "qn", "gTp", "xT", "w2t", "rec", "mcl", "gT", "split", "fin", "store", "stt", "red", "ncl",
+RANK = ["w1t", "sv", "L1", "L2", "r2", "qn", "gTp", "xT", "w2t", "rec", "mcl", "gT", "split", "fin", "finV", "store", "storeV", "stt", "red", "ncl",
         "w1q", "w2q", "H3", "X3", "X1", "H2", "X2", "gam", "msq", "w1c", "H1", "Sq", "Id", "Sqa", "w2c"]
-ONCE = ["w1t", "w1c", "w1q", "w2t", "w2c", "w2q"]
+ONCE = ["sv", "w1t", "w1c", "w1q", "w2t", "w2c", "w2q"]
 
 
 def regroup(nc, dst, src):
@@ -73,6 +74,16 @@ def tile_mlp_t_kernel(tc, x, in_mean, in_std, out_mean, out_std, W1, b1, W2, b2,
         warm2 = keep.tile([P, 1], F32)
         nc.scalar.activation(out=warm2[:], in_=warm[:], func=ACT.Sqrt)
 
+        W1v = W1.rearrange("(m p) k -> p m k", p=P)
+        W1n = []
+        for mm in range(4):
+            w1piece = keep.tile([P, 2, D_IN], BF16, name="w1piece%d" % mm)
+            W1n.append(w1piece)
+
+        def load_w1(mm):
+            nc.sync.dma_start(out=W1n[mm][:], in_=W1v[:, 2 * mm:2 * mm + 2, :])
+
+        load_w1(0)
         sv = keep.tile([P, P], BF16)
         nc.vector.memset(sv[:], 0.0)
         nc.sync.dma_start(out=sv[0:8, :], in_=b1.rearrange("(r c) -> r c", c=P))
@@ -86,11 +97,6 @@ def tile_mlp_t_kernel(tc, x, in_mean, in_std, out_mean, out_std, W1, b1, W2, b2,
         ident_f = keep.tile([P, P], F32)
         make_identity(nc, ident_f[:])
 
-        W1v = W1.rearrange("(m p) k -> p m k", p=P)
-        W1n = []
-        for mm in range(4):
-            w1piece = keep.tile([P, 2, D_IN], BF16, name="w1piece%d" % mm)
-            W1n.append(w1piece)
         W2v = W2.rearrange("(a p) k -> p a k", p=P)
         W2n = []
         for jp in range(2):
@@ -107,10 +113,6 @@ def tile_mlp_t_kernel(tc, x, in_mean, in_std, out_mean, out_std, W1, b1, W2, b2,
                 in_=x[c * CH:(c + 1) * CH, :].rearrange("(p i) k -> p i k", i=NI),
             )
 
-        def load_w1(mm):
-            nc.sync.dma_start(out=W1n[mm][:], in_=W1v[:, 2 * mm:2 * mm + 2, :])
-
-        load_w1(0)
         load_x(0)
         load_w1(1)
         load_w1(2)
@@ -132,14 +134,16 @@ def tile_mlp_t_kernel(tc, x, in_mean, in_std, out_mean, out_std, W1, b1, W2, b2,
             nc.vector.memset(gc[:], 0.0)
             gcols.append(gc)
 
-        svT = psum.tile([P, P], BF16, tag="qn", bufs=2)
-        nc.tensor.transpose(svT[:], sv[:], ident_bf[:])
         svc = keep.tile([P, 24], F32)
-        nc.vector.tensor_copy(out=svc[:], in_=svT[:, 0:24])
         rstd = keep.tile([P, 4], F32)
-        nc.vector.reciprocal(rstd[:], svc[:, 12:16])
         sb2 = keep.tile([P, 4], F32)
-        nc.vector.tensor_mul(out=sb2[:], in0=svc[:, 16:20], in1=svc[:, 20:24])
+
+        def e_sv(c, k):
+            svT = psum.tile([P, P], BF16, tag="qn", bufs=2)
+            nc.tensor.transpose(svT[:], sv[:], ident_bf[:])
+            nc.vector.tensor_copy(out=svc[:], in_=svT[:, 0:24])
+            nc.vector.reciprocal(rstd[:], svc[:, 12:16])
+            nc.vector.tensor_mul(out=sb2[:], in0=svc[:, 16:20], in1=svc[:, 20:24])
 
         gW1 = keep.tile([P, D_HID, 4], BF16, align_bytes=64)
         W1q = keep.tile([P, D_HID], U32, align_bytes=64)
@@ -270,7 +274,7 @@ def tile_mlp_t_kernel(tc, x, in_mean, in_std, out_mean, out_std, W1, b1, W2, b2,
             if jt == 0:
                 qT = work.tile([P, 4, CH], F32, tag="qT", bufs=4)
                 T["qT", c] = qT
-            if jt in ID_ON_VECTOR:
+            if jt in ID_ON_VECTOR or c == NCH - 1:
                 nc.vector.tensor_scalar(
                     out=T["qT", c][:, jt, :], in0=T["pt", c, jt][:],
                     scalar1=svc[:, 20 + jt:21 + jt], scalar2=sb2[:, jt:jt + 1], op0=ALU.mult, op1=ALU.add,
@@ -336,7 +340,7 @@ def tile_mlp_t_kernel(tc, x, in_mean, in_std, out_mean, out_std, W1, b1, W2, b2,
 
         def e_stt(c, i):
             if i == 0:
-                mp = work.tile([P, NI, D_OUT], F32, tag="mp", bufs=3)
+                mp = work.tile([P, NI, D_OUT], F32, tag="mp", bufs=4)
                 m2 = work.tile([P, NI], F32, tag="m2", bufs=3)
                 T["mp", c] = mp
                 T["m2", c] = m2
@@ -371,6 +375,9 @@ def tile_mlp_t_kernel(tc, x, in_mean, in_std, out_mean, out_std, W1, b1, W2, b2,
                 op0=ALU.mult, op1=ALU.add,
             )
 
+        def e_finV(c, i):
+            nc.vector.tensor_scalar_mul(out=T["mp", c][:, i, :], in0=T["mp", c][:, i, :], scalar1=T["beta", c][:, i:i + 1])
+
         def e_store(c, k):
             nc.sync.dma_start(
                 out=out[c * CH:(c + 1) * CH, :].rearrange("(p i) j -> p i j", i=NI),
@@ -378,15 +385,17 @@ def tile_mlp_t_kernel(tc, x, in_mean, in_std, out_mean, out_std, W1, b1, W2, b2,
             )
 
         emit = {
-            "w1t": e_w1t, "w1c": e_w1c, "w1q": e_w1q, "w2t": e_w2t, "w2c": e_w2c, "w2q": e_w2q,
+            "sv": e_sv, "w1t": e_w1t, "w1c": e_w1c, "w1q": e_w1q, "w2t": e_w2t, "w2c": e_w2c, "w2q": e_w2q,
             "xT": e_xT, "X1": e_X1, "X2": e_X2, "X3": e_X3, "L1": e_L1, "H1": e_H1, "H2": e_H2, "H3": e_H3,
             "L2": e_L2, "Sq": e_Sq, "Id": e_Id, "r2": e_r2, "red": e_red, "ncl": e_ncl, "gam": e_gam, "split": e_split,
             "gTp": e_gTp, "gT": e_gT, "qn": e_qn, "stt": e_stt, "Sqa": e_Sqa, "mcl": e_mcl, "msq": e_msq,
-            "rec": e_rec, "fin": e_fin, "store": e_store,
+            "rec": e_rec, "fin": e_fin, "store": e_store, "finV": e_finV, "storeV": e_store,
         }
         events = []
         for kind in RANK:
             for c in range(1 if kind in ONCE else NCH):
+                if (kind in ("fin", "store") and c in VFIN) or (kind in ("finV", "storeV") and c not in VFIN):
+                    continue
                 for k in range(len(STEPS[kind])):
                     events.append((PERIOD * c + STEPS[kind][k], RANK.index(kind), c, k, kind))
         if PIN:

@@ -26,22 +26,22 @@ EPS = 1e-12
 NPIECE = 3
 PERIOD = 8
 PIN = True
-ID_ON_VECTOR = [3]
-VFIN = [NCH - 2, NCH - 1]
+ID_ON_VECTOR = [1, 3]
+VFIN = [NCH - 3, NCH - 2, NCH - 1]
 
 STEPS = {
     "sv": [0], "w1t": [0, 1, 2, 3], "w1c": [1, 2, 3, 4], "w1q": [5, 7],
     "w2t": [9, 11, 13, 15], "w2c": [10, 12, 14, 16], "w2q": [14, 18],
-    "xT": [0, 2], "X1": [1, 3], "X2": [4], "X3": [6],
-    "L1": [7, 8, 9, 10, 11, 12, 13, 14], "H1": [8, 9, 10, 11, 12, 13, 14, 15],
-    "H2": [14, 18], "H3": [16, 20],
-    "L2": [22, 24, 26, 28], "Sq": [23, 25, 27, 29], "Id": [24, 26, 28, 30], "r2": [25, 27, 29, 31],
-    "red": [32], "ncl": [33], "gam": [35], "split": [36], "gTp": [38], "gT": [39],
-    "qn": [41, 43, 45, 47], "stt": [42, 44, 46, 48], "Sqa": [44, 46, 48, 50],
-    "mcl": [52], "msq": [54], "rec": [56], "fin": [61, 62, 63, 64], "store": [65], "finV": [57, 58, 59, 60], "storeV": [61],
+    "xT": [0, 2], "X1": [1, 3], "X2": [4], "X3": [8],
+    "L1": [9, 10, 11, 12, 13, 14, 15, 16], "H1": [10, 11, 12, 13, 14, 15, 16, 17],
+    "H2": [16, 20], "H3": [18, 22],
+    "L2": [24, 26, 28, 30], "Sq": [25, 27, 29, 31], "Id": [26, 28, 30, 32], "r2": [27, 29, 31, 33],
+    "red": [34], "ncl": [35], "gam": [37], "split": [38], "gTp": [42], "gT": [43],
+    "qn": [44, 46, 48, 50], "stt": [45, 47, 49, 51], "Sqa": [47, 49, 51, 53],
+    "mcl": [55], "msq": [57], "rec": [59], "fin": [62, 63, 64, 65], "store": [67], "finV": [60, 61, 62, 63], "storeV": [64],
 }
-RANK = ["w1t", "sv", "L1", "L2", "r2", "qn", "gTp", "xT", "w2t", "rec", "mcl", "gT", "split", "fin", "finV", "store", "storeV", "stt", "red", "ncl",
-        "w1q", "w2q", "H3", "X3", "X1", "H2", "X2", "gam", "msq", "w1c", "H1", "Sq", "Id", "Sqa", "w2c"]
+RANK = ["w1t", "sv", "L1", "L2", "r2", "qn", "gTp", "xT", "w2t", "rec", "mcl", "gT", "split", "ncl", "X2", "fin", "finV", "store", "storeV",
+        "stt", "red", "w1q", "w2q", "H3", "X3", "X1", "H2", "gam", "msq", "w1c", "H1", "Sq", "Id", "Sqa", "w2c"]
 ONCE = ["sv", "w1t", "w1c", "w1q", "w2t", "w2c", "w2q"]
 
 
@@ -182,10 +182,7 @@ def tile_mlp_t_kernel(tc, x, in_mean, in_std, out_mean, out_std, W1, b1, W2, b2,
             g, jp = u // 2, u % 2
             dst2 = gW2[:, g, 256 * jp:256 * (jp + 1), :].rearrange("p (m r) t -> p m r t", m=2)
             src2 = T["wt2", u][:].rearrange("p m t r -> p m r t")
-            if jp == 0:
-                nc.scalar.copy(out=dst2, in_=src2)
-            else:
-                nc.vector.tensor_copy(out=dst2, in_=src2)
+            nc.scalar.copy(out=dst2, in_=src2)
 
         def e_w2q(c, g):
             quantise(nc, W2q[:, g, :], W2s[:, g, :], gW2[:, g, :, :])
@@ -215,7 +212,13 @@ def tile_mlp_t_kernel(tc, x, in_mean, in_std, out_mean, out_std, W1, b1, W2, b2,
         def e_X2(c, k):
             gx = work.tile([P, CH, 4], BF16, tag="gx", bufs=2, align_bytes=64)
             T["gx", c] = gx
-            regroup(nc, gx[:], T["sx", c][:])
+            if c == 0:
+                regroup(nc, gx[:], T["sx", c][:])
+            else:
+                nc.gpsimd.tensor_scalar(
+                    out=gx[:], in0=T["sx", c][:].rearrange("p t n -> p n t"), scalar1=1.0, scalar2=0.0,
+                    op0=ALU.mult, op1=ALU.add,
+                )
 
         def e_X3(c, k):
             xq = work.tile([P, CH], U32, tag="xq", bufs=2, align_bytes=64)
@@ -319,7 +322,7 @@ def tile_mlp_t_kernel(tc, x, in_mean, in_std, out_mean, out_std, W1, b1, W2, b2,
                     rest = nrest
 
         def e_gTp(c, k):
-            gTp = psum.tile([P, P], BF16, tag="xT", bufs=1)
+            gTp = psum.tile([P, P], BF16, tag="qn", bufs=2)
             T["gTp", c] = gTp
             nc.tensor.transpose(gTp[:], gcols[c % 2][:], ident_bf[:])
 

@@ -25,14 +25,14 @@ NI = CH // P
 EPS = 1e-12
 NPIECE = 3
 PERIOD = 8
-PIN = True
-ID_ON_VECTOR = [1, 3]
-VFIN = [NCH - 3, NCH - 2, NCH - 1]
+PIN = False
+ID_ON_VECTOR = []
+VFIN = [0, 1, 2, 3, 4, 5, 6, 7]
 
 STEPS = {
-    "sv": [0], "w1t": [0, 1, 2, 3], "w1c": [1, 2, 3, 4], "w1q": [5, 7],
-    "w2t": [9, 11, 13, 15], "w2c": [10, 12, 14, 16], "w2q": [14, 18],
-    "xT": [0, 2], "X1": [1, 3], "X2": [4], "X3": [8],
+    "sv": [0], "w1t": [1, 3, 9, 11], "w1c": [2, 4, 11, 13], "w1q": [6, 8, 12, 14],
+    "w2t": [13, 15, 17, 19], "w2c": [14, 16, 18, 20], "w2q": [17, 22],
+    "xT": [0, 2], "X1": [1, 3], "X2": [5], "X3": [7],
     "L1": [9, 10, 11, 12, 13, 14, 15, 16], "H1": [10, 11, 12, 13, 14, 15, 16, 17],
     "H2": [16, 20], "H3": [18, 22],
     "L2": [24, 26, 28, 30], "Sq": [25, 27, 29, 31], "Id": [26, 28, 30, 32], "r2": [27, 29, 31, 33],
@@ -40,7 +40,7 @@ STEPS = {
     "qn": [44, 46, 48, 50], "stt": [45, 47, 49, 51], "Sqa": [47, 49, 51, 53],
     "mcl": [55], "msq": [57], "rec": [59], "fin": [62, 63, 64, 65], "store": [67], "finV": [60, 61, 62, 63], "storeV": [64],
 }
-RANK = ["w1t", "sv", "L1", "L2", "r2", "qn", "gTp", "xT", "w2t", "rec", "mcl", "gT", "split", "ncl", "X2", "fin", "finV", "store", "storeV",
+RANK = ["sv", "L1", "L2", "r2", "qn", "gTp", "xT", "w1t", "w2t", "rec", "mcl", "gT", "split", "ncl", "X2", "fin", "finV", "store", "storeV",
         "stt", "red", "w1q", "w2q", "H3", "X3", "X1", "H2", "gam", "msq", "w1c", "H1", "Sq", "Id", "Sqa", "w2c"]
 ONCE = ["sv", "w1t", "w1c", "w1q", "w2t", "w2c", "w2q"]
 
@@ -83,7 +83,18 @@ def tile_mlp_t_kernel(tc, x, in_mean, in_std, out_mean, out_std, W1, b1, W2, b2,
         def load_w1(mm):
             nc.sync.dma_start(out=W1n[mm][:], in_=W1v[:, 2 * mm:2 * mm + 2, :])
 
-        load_w1(0)
+        xs_all = []
+        for c in range(NCH):
+            xs = xpool.tile([P, NI, D_IN], BF16)
+            xs_all.append(xs)
+
+        def load_x(c):
+            nc.sync.dma_start(
+                out=xs_all[c][:],
+                in_=x[c * CH:(c + 1) * CH, :].rearrange("(p i) k -> p i k", i=NI),
+            )
+
+        load_x(0)
         sv = keep.tile([P, P], BF16)
         nc.vector.memset(sv[:], 0.0)
         nc.sync.dma_start(out=sv[0:8, :], in_=b1.rearrange("(r c) -> r c", c=P))
@@ -102,18 +113,7 @@ def tile_mlp_t_kernel(tc, x, in_mean, in_std, out_mean, out_std, W1, b1, W2, b2,
         for jp in range(2):
             w2piece = keep.tile([P, 2, D_HID], BF16, name="w2piece%d" % jp)
             W2n.append(w2piece)
-        xs_all = []
-        for c in range(NCH):
-            xs = xpool.tile([P, NI, D_IN], BF16)
-            xs_all.append(xs)
-
-        def load_x(c):
-            nc.sync.dma_start(
-                out=xs_all[c][:],
-                in_=x[c * CH:(c + 1) * CH, :].rearrange("(p i) k -> p i k", i=NI),
-            )
-
-        load_x(0)
+        load_w1(0)
         load_w1(1)
         load_w1(2)
         load_w1(3)
@@ -156,7 +156,7 @@ def tile_mlp_t_kernel(tc, x, in_mean, in_std, out_mean, out_std, W1, b1, W2, b2,
         T = {}
 
         def e_w1t(c, mm):
-            wt = psum.tile([P, 2, 4, P], BF16, tag=("l1" if mm % 2 == 0 else "pt"), bufs=2)
+            wt = psum.tile([P, 2, 4, P], BF16, tag="pt", bufs=2)
             T["wt", mm] = wt
             for m2 in range(2):
                 for t in range(4):
@@ -166,8 +166,8 @@ def tile_mlp_t_kernel(tc, x, in_mean, in_std, out_mean, out_std, W1, b1, W2, b2,
             dst = gW1[:, 256 * mm:256 * (mm + 1), :].rearrange("p (m r) t -> p m r t", m=2)
             nc.scalar.copy(out=dst, in_=T["wt", mm][:].rearrange("p m t r -> p m r t"))
 
-        def e_w1q(c, h):
-            quantise(nc, W1q[:, 512 * h:512 * (h + 1)], W1s[:, 512 * h:512 * (h + 1)], gW1[:, 512 * h:512 * (h + 1), :])
+        def e_w1q(c, mm):
+            quantise(nc, W1q[:, 256 * mm:256 * (mm + 1)], W1s[:, 256 * mm:256 * (mm + 1)], gW1[:, 256 * mm:256 * (mm + 1), :])
 
         def e_w2t(c, u):
             g, jp = u // 2, u % 2
@@ -212,7 +212,7 @@ def tile_mlp_t_kernel(tc, x, in_mean, in_std, out_mean, out_std, W1, b1, W2, b2,
         def e_X2(c, k):
             gx = work.tile([P, CH, 4], BF16, tag="gx", bufs=2, align_bytes=64)
             T["gx", c] = gx
-            if c == 0:
+            if c >= 0:
                 regroup(nc, gx[:], T["sx", c][:])
             else:
                 nc.gpsimd.tensor_scalar(
@@ -277,7 +277,7 @@ def tile_mlp_t_kernel(tc, x, in_mean, in_std, out_mean, out_std, W1, b1, W2, b2,
             if jt == 0:
                 qT = work.tile([P, 4, CH], F32, tag="qT", bufs=4)
                 T["qT", c] = qT
-            if jt in ID_ON_VECTOR or c == NCH - 1:
+            if jt in ID_ON_VECTOR:
                 nc.vector.tensor_scalar(
                     out=T["qT", c][:, jt, :], in0=T["pt", c, jt][:],
                     scalar1=svc[:, 20 + jt:21 + jt], scalar2=sb2[:, jt:jt + 1], op0=ALU.mult, op1=ALU.add,

from contextlib import ExitStack

import concourse.mybir as mybir
from concourse.masks import make_identity

FLOPS = 2 * 4096 * (512 * 1024 + 1024 * 512)

BF16 = mybir.dt.bfloat16
F32 = mybir.dt.float32
U32 = mybir.dt.uint32
U8 = mybir.dt.uint8
FP8X4 = mybir.dt.float8_e4m3fn_x4
ALU = mybir.AluOpType
ACT = mybir.ActivationFunctionType
AX = mybir.AxisListType

P = 128
B = 4096
D_IN = 512
D_HID = 1024
D_OUT = 512
CH = 512
NCH = B // CH
NI = CH // P
EPS = 1e-12
NPIECE = 3
PERIOD = 8
PIN = False
ID_ON_VECTOR = []
VFIN = [0, 1, 2, 3, 4, 5, 6, 7]

STEPS = {
    "sv": [0], "w1t": [1, 3, 9, 11], "w1c": [2, 4, 11, 13], "w1q": [6, 8, 12, 14],
    "w2t": [13, 15, 17, 19], "w2c": [14, 16, 18, 20], "w2q": [17, 22],
    "xT": [0, 2], "X1": [1, 3], "X2": [5], "X3": [7],
    "L1": [9, 10, 11, 12, 13, 14, 15, 16], "H1": [10, 11, 12, 13, 14, 15, 16, 17],
    "H2": [16, 20], "H3": [18, 22],
    "L2": [24, 26, 28, 30], "Sq": [25, 27, 29, 31], "Id": [26, 28, 30, 32], "r2": [27, 29, 31, 33],
    "red": [34], "ncl": [35], "gam": [37], "split": [38], "gTp": [42], "gT": [43],
    "qn": [44, 46, 48, 50], "stt": [45, 47, 49, 51], "Sqa": [47, 49, 51, 53],
    "mcl": [55], "msq": [57], "rec": [59], "fin": [62, 63, 64, 65], "store": [67], "finV": [60, 61, 62, 63], "storeV": [64],
}
RANK = ["sv", "L1", "L2", "r2", "qn", "gTp", "xT", "w1t", "w2t", "rec", "mcl", "gT", "split", "ncl", "X2", "fin", "finV", "store", "storeV",
        "stt", "red", "w1q", "w2q", "H3", "X3", "X1", "H2", "gam", "msq", "w1c", "H1", "Sq", "Id", "Sqa", "w2c"]
ONCE = ["sv", "w1t", "w1c", "w1q", "w2t", "w2c", "w2q"]


def regroup(nc, dst, src):
    nc.vector.tensor_copy(
        out=dst.rearrange("p (c i) t -> p c t i", i=4),
        in_=src.rearrange("p t (c i) -> p c t i", i=4),
    )


def quantise(nc, codes, scales, grouped):
    nc.vector.quantize_mx(
        out=codes.bitcast(FP8X4),
        scales=scales,
        in_=grouped.rearrange("p n t -> p (n t)"),
    )


def tile_mlp_t_kernel(tc, x, in_mean, in_std, out_mean, out_std, W1, b1, W2, b2, norm_max, out):
    nc = tc.nc
    nm2 = float(norm_max) * float(norm_max)
    with ExitStack() as ctx:
        keep = ctx.enter_context(tc.tile_pool(name="keep", bufs=1))
        xpool = ctx.enter_context(tc.tile_pool(name="xpool", bufs=NCH))
        work = ctx.enter_context(tc.tile_pool(name="work", bufs=2))
        psum = ctx.enter_context(tc.psum_pool(name="psum", bufs=1))

        warm = keep.tile([P, 1], F32)
        nc.vector.memset(warm[:], 1.0)
        warm2 = keep.tile([P, 1], F32)
        nc.scalar.activation(out=warm2[:], in_=warm[:], func=ACT.Sqrt)

        W1v = W1.rearrange("(m p) k -> p m k", p=P)
        W1n = []
        for mm in range(4):
            w1piece = keep.tile([P, 2, D_IN], BF16, name="w1piece%d" % mm)
            W1n.append(w1piece)

        def load_w1(mm):
            nc.sync.dma_start(out=W1n[mm][:], in_=W1v[:, 2 * mm:2 * mm + 2, :])

        xs_all = []
        for c in range(NCH):
            xs = xpool.tile([P, NI, D_IN], BF16)
            xs_all.append(xs)

        def load_x(c):
            nc.sync.dma_start(
                out=xs_all[c][:],
                in_=x[c * CH:(c + 1) * CH, :].rearrange("(p i) k -> p i k", i=NI),
            )

        load_x(0)
        sv = keep.tile([P, P], BF16)
        nc.vector.memset(sv[:], 0.0)
        nc.sync.dma_start(out=sv[0:8, :], in_=b1.rearrange("(r c) -> r c", c=P))
        nc.sync.dma_start(out=sv[8:12, :], in_=in_mean.rearrange("(r c) -> r c", c=P))
        nc.sync.dma_start(out=sv[12:16, :], in_=in_std.rearrange("(r c) -> r c", c=P))
        nc.sync.dma_start(out=sv[16:20, :], in_=b2.rearrange("(r c) -> r c", c=P))
        nc.sync.dma_start(out=sv[20:24, :], in_=out_std.rearrange("(r c) -> r c", c=P))

        ident_bf = keep.tile([P, P], BF16)
        make_identity(nc, ident_bf[:])
        ident_f = keep.tile([P, P], F32)
        make_identity(nc, ident_f[:])

        W2v = W2.rearrange("(a p) k -> p a k", p=P)
        W2n = []
        for jp in range(2):
            w2piece = keep.tile([P, 2, D_HID], BF16, name="w2piece%d" % jp)
            W2n.append(w2piece)
        load_w1(0)
        load_w1(1)
        load_w1(2)
        load_w1(3)
        load_x(1)
        for jp in range(2):
            nc.sync.dma_start(out=W2n[jp][:], in_=W2v[:, 2 * jp:2 * jp + 2, :])
        for c in range(2, NCH):
            load_x(c)

        shift = keep.tile([P, NI, D_OUT], BF16)
        nc.vector.memset(shift[:], 0.0)
        for i in range(NI):
            nc.sync.dma_start(out=shift[4 * i:4 * i + 4, i, :], in_=out_mean.partition_broadcast(4))
            nc.sync.dma_start(out=shift[32 + 4 * i:32 + 4 * i + 4, i, :], in_=in_mean.partition_broadcast(4))
        gcols = []
        for bb in range(2):
            gc = keep.tile([P, P], BF16, name="gcols%d" % bb)
            nc.vector.memset(gc[:], 0.0)
            gcols.append(gc)

        svc = keep.tile([P, 24], F32)
        rstd = keep.tile([P, 4], F32)
        sb2 = keep.tile([P, 4], F32)

        def e_sv(c, k):
            svT = psum.tile([P, P], BF16, tag="qn", bufs=2)
            nc.tensor.transpose(svT[:], sv[:], ident_bf[:])
            nc.vector.tensor_copy(out=svc[:], in_=svT[:, 0:24])
            nc.vector.reciprocal(rstd[:], svc[:, 12:16])
            nc.vector.tensor_mul(out=sb2[:], in0=svc[:, 16:20], in1=svc[:, 20:24])

        gW1 = keep.tile([P, D_HID, 4], BF16, align_bytes=64)
        W1q = keep.tile([P, D_HID], U32, align_bytes=64)
        W1s = keep.tile([P, D_HID], U8, align_bytes=64)
        W2q = keep.tile([P, 2, D_OUT], U32, align_bytes=64)
        W2s = keep.tile([P, 2, D_OUT], U8, align_bytes=64)
        gW2 = keep.tile([P, 2, D_OUT, 4], BF16, align_bytes=64)
        junk = keep.tile([P, D_OUT], F32)

        T = {}

        def e_w1t(c, mm):
            wt = psum.tile([P, 2, 4, P], BF16, tag="pt", bufs=2)
            T["wt", mm] = wt
            for m2 in range(2):
                for t in range(4):
                    nc.tensor.transpose(wt[:, m2, t, :], W1n[mm][:, m2, t * P:(t + 1) * P], ident_bf[:])

        def e_w1c(c, mm):
            dst = gW1[:, 256 * mm:256 * (mm + 1), :].rearrange("p (m r) t -> p m r t", m=2)
            nc.scalar.copy(out=dst, in_=T["wt", mm][:].rearrange("p m t r -> p m r t"))

        def e_w1q(c, mm):
            quantise(nc, W1q[:, 256 * mm:256 * (mm + 1)], W1s[:, 256 * mm:256 * (mm + 1)], gW1[:, 256 * mm:256 * (mm + 1), :])

        def e_w2t(c, u):
            g, jp = u // 2, u % 2
            wt2 = psum.tile([P, 2, 4, P], BF16, tag="pt", bufs=2)
            T["wt2", u] = wt2
            for j2 in range(2):
                for t in range(4):
                    k0 = 512 * g + P * t
                    nc.tensor.transpose(wt2[:, j2, t, :], W2n[jp][:, j2, k0:k0 + P], ident_bf[:])

        def e_w2c(c, u):
            g, jp = u // 2, u % 2
            dst2 = gW2[:, g, 256 * jp:256 * (jp + 1), :].rearrange("p (m r) t -> p m r t", m=2)
            src2 = T["wt2", u][:].rearrange("p m t r -> p m r t")
            nc.scalar.copy(out=dst2, in_=src2)

        def e_w2q(c, g):
            quantise(nc, W2q[:, g, :], W2s[:, g, :], gW2[:, g, :, :])
            if g == 1:
                nc.vector.tensor_scalar_mul(out=shift[32:64, :, :], in0=shift[32:64, :, :], scalar1=-1.0)

        def e_xT(c, th):
            xT = psum.tile([P, 2, CH], BF16, tag="xT", bufs=1)
            T["xT", c, th] = xT
            for t2 in range(2):
                t = 2 * th + t2
                for i in range(NI):
                    nc.tensor.transpose(xT[:, t2, i * P:(i + 1) * P], xs_all[c][:, i, t * P:(t + 1) * P], ident_bf[:])

        def e_X1(c, th):
            if th == 0:
                sx = work.tile([P, 4, CH], BF16, tag="sx", bufs=2)
                T["sx", c] = sx
            for t2 in range(2):
                t = 2 * th + t2
                nc.vector.tensor_scalar(
                    out=T["sx", c][:, t, :], in0=T["xT", c, th][:, t2, :],
                    scalar1=svc[:, 8 + t:9 + t], scalar2=rstd[:, t:t + 1],
                    op0=ALU.subtract, op1=ALU.mult,
                )

        def e_X2(c, k):
            gx = work.tile([P, CH, 4], BF16, tag="gx", bufs=2, align_bytes=64)
            T["gx", c] = gx
            if c >= 0:
                regroup(nc, gx[:], T["sx", c][:])
            else:
                nc.gpsimd.tensor_scalar(
                    out=gx[:], in0=T["sx", c][:].rearrange("p t n -> p n t"), scalar1=1.0, scalar2=0.0,
                    op0=ALU.mult, op1=ALU.add,
                )

        def e_X3(c, k):
            xq = work.tile([P, CH], U32, tag="xq", bufs=2, align_bytes=64)
            xsc = work.tile([P, CH], U8, tag="xsc", bufs=2, align_bytes=64)
            T["xq", c] = xq
            T["xsc", c] = xsc
            quantise(nc, xq[:], xsc[:], T["gx", c][:])

        def e_L1(c, m):
            l1 = psum.tile([P, CH], F32, tag="l1", bufs=2)
            T["l1", c, m] = l1
            nc.tensor.matmul_mx(
                out=l1[:],
                lhsT=W1q[:, m * P:(m + 1) * P].bitcast(FP8X4), lhsT_scale=W1s[:, m * P:(m + 1) * P],
                rhs=T["xq", c][:].bitcast(FP8X4), rhs_scale=T["xsc", c][:],
                start=True, stop=True,
            )

        def e_H1(c, m):
            if m % 4 == 0:
                sh = work.tile([P, 4, CH], BF16, tag="sh", bufs=3)
                T["sh", c, m // 4] = sh
            nc.scalar.activation(out=T["sh", c, m // 4][:, m % 4, :], in_=T["l1", c, m][:], func=ACT.Relu,
                                 bias=svc[:, m:m + 1], scale=1.0)

        def e_H2(c, g):
            gh = work.tile([P, CH, 4], BF16, tag="gh", bufs=2, align_bytes=64)
            T["gh", c, g] = gh
            regroup(nc, gh[:], T["sh", c, g][:])

        def e_H3(c, g):
            if g == 0:
                hq = work.tile([P, 2, CH], U32, tag="hq", bufs=2, align_bytes=64)
                hs = work.tile([P, 2, CH], U8, tag="hs", bufs=2, align_bytes=64)
                T["hq", c] = hq
                T["hs", c] = hs
            quantise(nc, T["hq", c][:, g, :], T["hs", c][:, g, :], T["gh", c, g][:])

        def e_L2(c, jt):
            pt = psum.tile([P, CH], F32, tag="pt", bufs=2)
            T["pt", c, jt] = pt
            for g in range(2):
                nc.tensor.matmul_mx(
                    out=pt[:],
                    lhsT=W2q[:, g, jt * P:(jt + 1) * P].bitcast(FP8X4), lhsT_scale=W2s[:, g, jt * P:(jt + 1) * P],
                    rhs=T["hq", c][:, g, :].bitcast(FP8X4), rhs_scale=T["hs", c][:, g, :],
                    start=(g == 0), stop=(g == 1),
                )

        def e_Sq(c, jt):
            r2T = work.tile([P, CH], F32, tag="r2T", bufs=3)
            T["r2T", c, jt] = r2T
            nc.scalar.activation(out=r2T[:], in_=T["pt", c, jt][:], func=ACT.Square, bias=svc[:, 16 + jt:17 + jt], scale=1.0)

        def e_Id(c, jt):
            if jt == 0:
                qT = work.tile([P, 4, CH], F32, tag="qT", bufs=4)
                T["qT", c] = qT
            if jt in ID_ON_VECTOR:
                nc.vector.tensor_scalar(
                    out=T["qT", c][:, jt, :], in0=T["pt", c, jt][:],
                    scalar1=svc[:, 20 + jt:21 + jt], scalar2=sb2[:, jt:jt + 1], op0=ALU.mult, op1=ALU.add,
                )
            else:
                nc.scalar.activation(out=T["qT", c][:, jt, :], in_=T["pt", c, jt][:], func=ACT.Identity,
                                     bias=sb2[:, jt:jt + 1], scale=svc[:, 20 + jt:21 + jt])

        def e_r2(c, jt):
            if jt == 0:
                r2b = psum.tile([P, CH], F32, tag="r2", bufs=1)
                T["r2b", c] = r2b
            for i in range(NI):
                nc.tensor.matmul(
                    out=T["r2b", c][:, i * P:(i + 1) * P], lhsT=T["r2T", c, jt][:, i * P:(i + 1) * P], rhs=ident_f[:],
                    is_transpose=True, start=(jt == 0 and i == 0), stop=(jt == 3 and i == NI - 1),
                )

        def e_red(c, k):
            n2 = work.tile([P, NI], F32, tag="n2", bufs=4)
            T["n2", c] = n2
            nc.vector.tensor_reduce(out=n2[:], in_=T["r2b", c][:].rearrange("p (i j) -> p i j", i=NI), axis=AX.X, op=ALU.add)

        def e_ncl(c, k):
            ncl = work.tile([P, NI], F32, tag="ncl", bufs=4)
            T["ncl", c] = ncl
            nc.gpsimd.tensor_scalar_max(out=ncl[:], in0=T["n2", c][:], scalar1=nm2)

        def e_gam(c, k):
            gam = work.tile([P, NI], F32, tag="gam", bufs=4)
            T["gam", c] = gam
            nc.scalar.activation(out=gam[:], in_=T["ncl", c][:], func=ACT.Sqrt, scale=1.0 / nm2)

        def e_split(c, k):
            gview = gcols[c % 2][:, 0:64].rearrange("p (s i a) -> p s i a", s=2, a=4)
            rest = T["gam", c]
            for a in range(NPIECE):
                nc.gpsimd.tensor_copy(out=gview[:, :, 0:NI, a], in_=rest[:].unsqueeze(1).to_broadcast([P, 2, NI]))
                if a < NPIECE - 1:
                    nrest = work.tile([P, NI], F32, tag="rest%d" % a, bufs=2)
                    nc.gpsimd.tensor_sub(out=nrest[:], in0=rest[:], in1=gview[:, 0, 0:NI, a])
                    rest = nrest

        def e_gTp(c, k):
            gTp = psum.tile([P, P], BF16, tag="qn", bufs=2)
            T["gTp", c] = gTp
            nc.tensor.transpose(gTp[:], gcols[c % 2][:], ident_bf[:])

        def e_gT(c, k):
            gT = work.tile([P, P], BF16, tag="gT", bufs=2)
            T["gT", c] = gT
            nc.vector.tensor_copy(out=gT[:], in_=T["gTp", c][:])

        def e_qn(c, i):
            qn = psum.tile([P, D_OUT], F32, tag="qn", bufs=2)
            T["qn", c, i] = qn
            for jt in range(4):
                nc.tensor.matmul(
                    out=qn[:, jt * P:(jt + 1) * P], lhsT=T["qT", c][:, jt, i * P:(i + 1) * P], rhs=ident_f[:],
                    is_transpose=True, start=(jt == 0), stop=False,
                )
            nc.tensor.matmul(out=qn[:], lhsT=T["gT", c][:], rhs=shift[:, i, :], start=False, stop=True)

        def e_stt(c, i):
            if i == 0:
                mp = work.tile([P, NI, D_OUT], F32, tag="mp", bufs=4)
                m2 = work.tile([P, NI], F32, tag="m2", bufs=3)
                T["mp", c] = mp
                T["m2", c] = m2
            nc.vector.scalar_tensor_tensor(
                out=T["mp", c][:, i, :], in0=xs_all[c][:, i, :], scalar=T["gam", c][:, i:i + 1], in1=T["qn", c, i][:],
                op0=ALU.mult, op1=ALU.add,
            )

        def e_Sqa(c, i):
            nc.scalar.activation(out=junk[:], in_=T["mp", c][:, i, :], func=ACT.Square, accum_out=T["m2", c][:, i:i + 1])

        def e_mcl(c, k):
            mcl = work.tile([P, NI], F32, tag="mcl", bufs=2)
            T["mcl", c] = mcl
            nc.vector.scalar_tensor_tensor(
                out=mcl[:], in0=T["ncl", c][:], scalar=EPS * EPS / nm2, in1=T["m2", c][:], op0=ALU.mult, op1=ALU.max,
            )

        def e_msq(c, k):
            msq = work.tile([P, NI], F32, tag="msq", bufs=2)
            T["msq", c] = msq
            nc.scalar.activation(out=msq[:], in_=T["mcl", c][:], func=ACT.Sqrt)

        def e_rec(c, k):
            beta = work.tile([P, NI], F32, tag="beta", bufs=2)
            T["beta", c] = beta
            nc.vector.reciprocal(beta[:], T["msq", c][:])

        def e_fin(c, i):
            nc.gpsimd.tensor_scalar(
                out=T["mp", c][:, i, :], in0=T["mp", c][:, i, :], scalar1=T["beta", c][:, i:i + 1], scalar2=0.0,
                op0=ALU.mult, op1=ALU.add,
            )

        def e_finV(c, i):
            nc.vector.tensor_scalar_mul(out=T["mp", c][:, i, :], in0=T["mp", c][:, i, :], scalar1=T["beta", c][:, i:i + 1])

        def e_store(c, k):
            nc.sync.dma_start(
                out=out[c * CH:(c + 1) * CH, :].rearrange("(p i) j -> p i j", i=NI),
                in_=T["mp", c][:],
            )

        emit = {
            "sv": e_sv, "w1t": e_w1t, "w1c": e_w1c, "w1q": e_w1q, "w2t": e_w2t, "w2c": e_w2c, "w2q": e_w2q,
            "xT": e_xT, "X1": e_X1, "X2": e_X2, "X3": e_X3, "L1": e_L1, "H1": e_H1, "H2": e_H2, "H3": e_H3,
            "L2": e_L2, "Sq": e_Sq, "Id": e_Id, "r2": e_r2, "red": e_red, "ncl": e_ncl, "gam": e_gam, "split": e_split,
            "gTp": e_gTp, "gT": e_gT, "qn": e_qn, "stt": e_stt, "Sqa": e_Sqa, "mcl": e_mcl, "msq": e_msq,
            "rec": e_rec, "fin": e_fin, "store": e_store, "finV": e_finV, "storeV": e_store,
        }
        events = []
        for kind in RANK:
            for c in range(1 if kind in ONCE else NCH):
                if (kind in ("fin", "store") and c in VFIN) or (kind in ("finV", "storeV") and c not in VFIN):
                    continue
                for k in range(len(STEPS[kind])):
                    events.append((PERIOD * c + STEPS[kind][k], RANK.index(kind), c, k, kind))
        if PIN:
            ctx.enter_context(tc.manual_schedule())
        for ev in sorted(events):
            emit[ev[4]](ev[2], ev[3])
